import numpy as np
import ml_dtypes


def mxq(x, axis, fmt="e4m3"):
    dtype, down = {"e4m3": (ml_dtypes.float8_e4m3fn, 7), "e5m2": (ml_dtypes.float8_e5m2, 14)}[fmt]
    v = np.moveaxis(np.asarray(x, np.float32).astype(ml_dtypes.bfloat16).astype(np.float64), axis, -1)
    blocks = v.reshape(v.shape[:-1] + (-1, 32))
    amax = np.abs(blocks).max(-1, keepdims=True)
    byte = np.maximum(np.where(amax > 0, np.frexp(amax)[1] - 1 + 127, 0) - down, 1)
    scale = np.exp2(byte - 127.0)
    codes = (blocks / scale).astype(np.float32).astype(dtype).astype(np.float64)
    return np.moveaxis((codes * scale).reshape(v.shape), -1, axis)


WIDE = False


def mx_kscale(k):
    if not WIDE:
        return np.ones(k)
    levels = np.array([10, -10, 5, -5, 0])
    a = np.random.permutation(np.resize(levels, k // 512 * 4)).reshape(k // 512, 4)
    idx = np.arange(k)
    return np.exp2(a[idx // 512, idx % 128 // 32])


BF16 = ml_dtypes.bfloat16


def bf(x):
    return np.asarray(x, np.float32).astype(BF16)


def f64(x):
    return np.asarray(x).astype(np.float64)


B, N, DIM, H, D, M = 2, 512, 1024, 16, 64, 16
HD = H * D


def sigmoid(v):
    return 1.0 / (1.0 + np.exp(-v))


def setup_inputs():
    s = mx_kscale(DIM)
    t = mx_kscale(HD)
    return {"attn_out": bf(np.random.standard_normal((B, H, N, D)) * 0.2 * t.reshape(H, 1, D)[None]),
            "hg_lin": bf(np.random.standard_normal((B, N, H))),
            "x": bf(np.random.standard_normal((B, N, DIM)) * s),
            "Wg": bf(np.random.standard_normal((DIM, HD)) / np.sqrt(DIM) / s[:, None]),
            "bg": bf(np.random.standard_normal(HD) * 0.3),
            "bhg": bf(np.random.standard_normal(H) * 0.3),
            "Wo": bf(np.random.standard_normal((HD, DIM)) * 3.0 / np.sqrt(HD) / t[:, None])}


def reference(attn_out, hg_lin, x, Wg, bg, bhg, Wo):
    head_gate = sigmoid(f64(hg_lin) + f64(bhg))
    o = f64(attn_out) * head_gate.transpose(0, 2, 1)[..., None]
    o = o.transpose(0, 2, 1, 3).reshape(B, N, HD)
    o = o * sigmoid((mxq(f64(x), 2, "e4m3") @ mxq(f64(Wg), 0, "e4m3")) + f64(bg))
    return mxq(o, 2, "e4m3") @ mxq(f64(Wo), 0, "e4m3")

@@ -1,0 +1,262 @@
+from contextlib import ExitStack
+
+import concourse.mybir as mybir
+from concourse.masks import make_identity
+
+FLOPS = 2 * 2 * 1024 * 1024 * 1024
+
+BF16 = mybir.dt.bfloat16
+F32 = mybir.dt.float32
+U32 = mybir.dt.uint32
+U8 = mybir.dt.uint8
+FP8X4 = mybir.dt.float8_e4m3fn_x4
+ACT = mybir.ActivationFunctionType
+ALU = mybir.AluOpType
+
+P = 128
+PACK = 4
+K_PASS = P * PACK
+B = 2
+N = 512
+J = N // P
+DIM = 1024
+H = 16
+D = 64
+HD = H * D
+PASSES = DIM // K_PASS
+BANK = 512
+PAIR = 2
+
+
+def tile_attention_pb_kernel(tc, attn_out, hg_lin, x, Wg, bg, bhg, Wo, out):
+    nc = tc.nc
+    with ExitStack() as stack:
+        keep = stack.enter_context(tc.tile_pool(name="keep", bufs=1))
+        work = stack.enter_context(tc.tile_pool(name="work", bufs=2))
+        psum = stack.enter_context(tc.psum_pool(name="psum", bufs=2))
+        stack.enter_context(tc.manual_schedule())
+
+        ident_f32 = keep.tile([P, P], F32, name="ident_f32")
+        make_identity(nc, ident_f32[:])
+        ident_bf16 = keep.tile([P, P], BF16, name="ident_bf16")
+        make_identity(nc, ident_bf16[:])
+        bg_rows = keep.tile([P, P], BF16, name="bg_rows")
+        nc.vector.memset(bg_rows[:], 0.0)
+
+        hg_sb = keep.tile([P, B, J * H], BF16, name="hg_sb")
+        nc.sync.dma_start(out=hg_sb[:], in_=hg_lin.rearrange("b (p j) h -> p b (j h)", j=J))
+        bhg_sb = keep.tile([P, H], BF16, name="bhg_sb")
+        nc.sync.dma_start(out=bhg_sb[:], in_=bhg.partition_broadcast(P))
+        nc.sync.dma_start(out=bg_rows[0 : HD // P, :], in_=bg.rearrange("(m p) -> m p", p=P))
+
+        x_sb = [keep.tile([P, J * DIM], BF16, name="x_sb%d" % b) for b in range(B)]
+        attn_sb = [keep.tile([P, H, J, D], BF16, name="attn_sb%d" % b) for b in range(B)]
+        wg_raw = keep.tile([P, PASSES, PACK, HD], BF16, name="wg_raw")
+        wo_raw = keep.tile([P, PASSES, PACK, DIM], BF16, name="wo_raw")
+
+        def load_x(b):
+            nc.sync.dma_start(out=x_sb[b][:], in_=x[b].rearrange("(p j) k -> p (j k)", j=J))
+
+        def load_attn(b):
+            nc.sync.dma_start(
+                out=attn_sb[b][:].rearrange("p h j d -> p h (j d)"),
+                in_=attn_out[b].rearrange("h (p j) d -> p h (j d)", j=J),
+            )
+
+        wg_view = Wg.rearrange("(g u q e) c -> g q u (e c)", g=PASSES, u=2, e=2)
+        wo_view = Wo.rearrange("(g t p) c -> g p t c", g=PASSES, t=PACK)
+
+        load_x(0)
+        for g in range(PASSES):
+            nc.sync.dma_start(
+                out=wg_raw[:, g].rearrange("q (u e) c -> q u (e c)", e=2), in_=wg_view[g]
+            )
+        load_attn(0)
+        load_x(1)
+        for g in range(PASSES):
+            nc.sync.dma_start(out=wo_raw[:, g], in_=wo_view[g])
+        load_attn(1)
+
+        hg_sum = keep.tile([P, B * J, H], F32, name="hg_sum")
+        nc.vector.tensor_tensor(
+            out=hg_sum[:],
+            in0=hg_sb[:].rearrange("p b (j h) -> p (b j) h", h=H),
+            in1=bhg_sb[:].unsqueeze(1).to_broadcast([P, B * J, H]),
+            op=ALU.add,
+        )
+        head_gate = keep.tile([P, B * J, H], F32, name="head_gate")
+        nc.scalar.activation(out=head_gate[:], in_=hg_sum[:], func=ACT.Sigmoid)
+
+        bg_t = psum.tile([P, P], BF16, tag="tr", bufs=3, name="bg_t")
+        nc.tensor.transpose(bg_t[:], bg_rows[:], ident_bf16[:])
+        bg_col = keep.tile([P, HD // P], F32, name="bg_col")
+        nc.vector.tensor_copy(out=bg_col[:], in_=bg_t[:, 0 : HD // P])
+
+        wg_codes = keep.tile([P, PASSES, HD], U32, name="wg_codes", align_bytes=64)
+        wg_scales = keep.tile([P, PASSES, HD], U8, name="wg_scales", align_bytes=64)
+        wo_codes = keep.tile([P, PASSES, DIM], U32, name="wo_codes", align_bytes=64)
+        wo_scales = keep.tile([P, PASSES, DIM], U8, name="wo_scales", align_bytes=64)
+        x_codes = [keep.tile([P, PASSES, N], U32, name="x_codes%d" % b, align_bytes=64) for b in range(B)]
+        x_scales = [keep.tile([P, PASSES, N], U8, name="x_scales%d" % b, align_bytes=64) for b in range(B)]
+
+        def quantise_weight(raw, codes, scales, scalar_halves):
+            pieces = [(half, g) for half in range(2) for g in range(PASSES)]
+            grouped = {}
+            for i in range(len(pieces) + 1):
+                if i < len(pieces):
+                    half, g = pieces[i]
+                    grouped[i] = work.tile(
+                        [P, BANK * PACK], BF16, tag="w_grp", bufs=4, align_bytes=64, name="w_grp"
+                    )
+                    dst = grouped[i][:].rearrange("p (c i t) -> p c t i", i=4, t=PACK)
+                    src = raw[:, g, :, half * BANK : (half + 1) * BANK].rearrange("p t (c i) -> p c t i", i=4)
+                    if half in scalar_halves:
+                        nc.scalar.copy(out=dst, in_=src)
+                    else:
+                        nc.vector.tensor_copy(out=dst, in_=src)
+                if i > 0:
+                    half, g = pieces[i - 1]
+                    cols = slice(half * BANK, (half + 1) * BANK)
+                    nc.vector.quantize_mx(
+                        out=codes[:, g, cols].bitcast(FP8X4), scales=scales[:, g, cols], in_=grouped[i - 1][:]
+                    )
+
+        x_grp = {}
+
+        def transpose_x(b):
+            words = x_sb[b][:].bitcast(F32)
+            for g in range(PASSES):
+                x_grp[(b, g)] = work.tile([P, N * PACK], BF16, tag="x_grp", align_bytes=64, name="x_grp")
+                grouped_words = x_grp[(b, g)][:].bitcast(F32)
+                for jp in range(J // 2):
+                    xt = psum.tile([P, BANK], F32, tag="tr", bufs=3, name="xt")
+                    for u in range(2):
+                        for jj in range(2):
+                            first = (2 * jp + jj) * (DIM // 2) + g * (K_PASS // 2) + u * P
+                            nc.tensor.transpose(
+                                xt[:, (2 * u + jj) * P : (2 * u + jj + 1) * P],
+                                words[:, first : first + P],
+                                ident_f32[:],
+                            )
+                    nc.scalar.copy(
+                        out=grouped_words[:, jp * BANK : (jp + 1) * BANK].rearrange("q (c u) -> q c u", u=2),
+                        in_=xt[:].rearrange("q (u c) -> q c u", u=2),
+                    )
+
+        def quantise_x(b):
+            for g in range(PASSES):
+                nc.vector.quantize_mx(
+                    out=x_codes[b][:, g, :].bitcast(FP8X4), scales=x_scales[b][:, g, :], in_=x_grp[(b, g)][:]
+                )
+
+        o_sb = {}
+
+        def gate_heads(b):
+            for j in range(J):
+                o_sb[(b, j)] = work.tile([P, HD], F32, tag="o_sb", bufs=B * J, name="o_sb")
+                if b == 0:
+                    nc.vector.tensor_tensor(
+                        out=o_sb[(b, j)][:].rearrange("p (h d) -> p h d", h=H),
+                        in0=attn_sb[b][:, :, j, :],
+                        in1=head_gate[:, b * J + j, :].unsqueeze(2).to_broadcast([P, H, D]),
+                        op=ALU.mult,
+                    )
+                else:
+                    for h in range(H):
+                        nc.scalar.activation(
+                            out=o_sb[(b, j)][:, h * D : (h + 1) * D],
+                            in_=attn_sb[b][:, h, j, :],
+                            func=ACT.Copy,
+                            scale=head_gate[:, b * J + j, h : h + 1],
+                        )
+
+        g_sb = {}
+
+        def feature_gate(b, g2):
+            g_sb[(b, g2)] = work.tile([P, PACK, N], F32, tag="g_sb", bufs=B * PASSES, name="g_sb")
+            for t in range(PACK):
+                m = g2 * PACK + t
+                rows = slice(m * P, (m + 1) * P)
+                z = psum.tile([P, N], F32, tag="z", bufs=3, name="z")
+                for g in range(PASSES):
+                    nc.tensor.matmul_mx(
+                        out=z[:],
+                        lhsT=wg_codes[:, g, rows].bitcast(FP8X4),
+                        lhsT_scale=wg_scales[:, g, rows],
+                        rhs=x_codes[b][:, g, :].bitcast(FP8X4),
+                        rhs_scale=x_scales[b][:, g, :],
+                        start=(g == 0),
+                        stop=(g == PASSES - 1),
+                    )
+                nc.scalar.activation(
+                    out=g_sb[(b, g2)][:, t, :], in_=z[:], func=ACT.Sigmoid, bias=bg_col[:, m : m + 1]
+                )
+
+        y_codes = {}
+        y_scales = {}
+
+        def gated_value(b, jp):
+            grouped = work.tile([P, PASSES * PAIR * P * PACK], BF16, tag="y_grp", align_bytes=64)
+            for g2 in range(PASSES):
+                for jj in range(PAIR):
+                    j = PAIR * jp + jj
+                    ot = psum.tile([P, BANK], F32, tag="tr", bufs=3, name="ot")
+                    for t in range(PACK):
+                        first = g2 * K_PASS + t * P
+                        nc.tensor.transpose(
+                            ot[:, t * P : (t + 1) * P], o_sb[(b, j)][:, first : first + P], ident_f32[:]
+                        )
+                    piece = (g2 * PAIR + jj) * P * PACK
+                    nc.vector.tensor_tensor(
+                        out=grouped[:, piece : piece + P * PACK].rearrange("p (c t) -> p c t", t=PACK),
+                        in0=ot[:].rearrange("p (t c) -> p c t", t=PACK),
+                        in1=g_sb[(b, g2)][:, :, j * P : (j + 1) * P].rearrange("p t c -> p c t"),
+                        op=ALU.mult,
+                    )
+            y_codes[(b, jp)] = keep.tile([P, PASSES * PAIR * P], U32, name="y_codes%d%d" % (b, jp), align_bytes=64)
+            y_scales[(b, jp)] = keep.tile([P, PASSES * PAIR * P], U8, name="y_scales%d%d" % (b, jp), align_bytes=64)
+            nc.vector.quantize_mx(
+                out=y_codes[(b, jp)][:].bitcast(FP8X4), scales=y_scales[(b, jp)][:], in_=grouped[:]
+            )
+
+        def project(b, jp):
+            out_view = out[b].rearrange("(p j) c -> p j c", j=J)
+            for jj in range(PAIR):
+                for half in range(DIM // BANK):
+                    cols = slice(half * BANK, (half + 1) * BANK)
+                    acc = psum.tile([P, BANK], F32, tag="acc", name="acc")
+                    for g2 in range(PASSES):
+                        toks = slice((g2 * PAIR + jj) * P, (g2 * PAIR + jj + 1) * P)
+                        nc.tensor.matmul_mx(
+                            out=acc[:],
+                            lhsT=y_codes[(b, jp)][:, toks].bitcast(FP8X4),
+                            lhsT_scale=y_scales[(b, jp)][:, toks],
+                            rhs=wo_codes[:, g2, cols].bitcast(FP8X4),
+                            rhs_scale=wo_scales[:, g2, cols],
+                            start=(g2 == 0),
+                            stop=(g2 == PASSES - 1),
+                        )
+                    res = work.tile([P, BANK], F32, tag="res", bufs=6)
+                    nc.scalar.copy(out=res[:], in_=acc[:])
+                    nc.sync.dma_start(out=out_view[:, PAIR * jp + jj, cols], in_=res[:])
+
+        transpose_x(0)
+        quantise_x(0)
+        quantise_weight(wg_raw, wg_codes, wg_scales, (1,))
+        feature_gate(0, 0)
+        feature_gate(0, 1)
+        transpose_x(1)
+        gate_heads(0)
+        quantise_x(1)
+        gated_value(0, 0)
+        feature_gate(1, 0)
+        feature_gate(1, 1)
+        quantise_weight(wo_raw, wo_codes, wo_scales, ())
+        gate_heads(1)
+        gated_value(0, 1)
+        project(0, 0)
+        gated_value(1, 0)
+        project(0, 1)
+        gated_value(1, 1)
+        project(1, 0)
+        project(1, 1)

@@ -19,13 +19,20 @@ K_PASS = P * PACK
 B = 2
 N = 512
 J = N // P
+TILES = B * J
 DIM = 1024
 H = 16
 D = 64
 HD = H * D
 PASSES = DIM // K_PASS
 BANK = 512
-PAIR = 2
+HALVES = DIM // BANK
+
+GATE_AHEAD = 4
+TRANSPOSE_AHEAD = 2
+QUANTISE_BEHIND = 1
+PROJECT_BEHIND = 2
+VECTOR_GATED_TILES = 2
 
 
 def tile_attention_pb_kernel(tc, attn_out, hg_lin, x, Wg, bg, bhg, Wo, out):
@@ -33,7 +40,7 @@ def tile_attention_pb_kernel(tc, attn_out, hg_lin, x, Wg, bg, bhg, Wo, out):
     with ExitStack() as stack:
         keep = stack.enter_context(tc.tile_pool(name="keep", bufs=1))
         work = stack.enter_context(tc.tile_pool(name="work", bufs=2))
-        psum = stack.enter_context(tc.psum_pool(name="psum", bufs=2))
+        psum = stack.enter_context(tc.psum_pool(name="psum", bufs=4))
         stack.enter_context(tc.manual_schedule())
 
         ident_f32 = keep.tile([P, P], F32, name="ident_f32")
@@ -71,23 +78,23 @@ def tile_attention_pb_kernel(tc, attn_out, hg_lin, x, Wg, bg, bhg, Wo, out):
             nc.sync.dma_start(
                 out=wg_raw[:, g].rearrange("q (u e) c -> q u (e c)", e=2), in_=wg_view[g]
             )
-        load_attn(0)
         load_x(1)
+        load_attn(0)
         for g in range(PASSES):
             nc.sync.dma_start(out=wo_raw[:, g], in_=wo_view[g])
         load_attn(1)
 
-        hg_sum = keep.tile([P, B * J, H], F32, name="hg_sum")
+        hg_sum = keep.tile([P, TILES, H], F32, name="hg_sum")
         nc.vector.tensor_tensor(
             out=hg_sum[:],
             in0=hg_sb[:].rearrange("p b (j h) -> p (b j) h", h=H),
-            in1=bhg_sb[:].unsqueeze(1).to_broadcast([P, B * J, H]),
+            in1=bhg_sb[:].unsqueeze(1).to_broadcast([P, TILES, H]),
             op=ALU.add,
         )
-        head_gate = keep.tile([P, B * J, H], F32, name="head_gate")
+        head_gate = keep.tile([P, TILES, H], F32, name="head_gate")
         nc.scalar.activation(out=head_gate[:], in_=hg_sum[:], func=ACT.Sigmoid)
 
-        bg_t = psum.tile([P, P], BF16, tag="tr", bufs=3, name="bg_t")
+        bg_t = psum.tile([P, P], BF16, tag="tr", name="bg_t")
         nc.tensor.transpose(bg_t[:], bg_rows[:], ident_bf16[:])
         bg_col = keep.tile([P, HD // P], F32, name="bg_col")
         nc.vector.tensor_copy(out=bg_col[:], in_=bg_t[:, 0 : HD // P])
@@ -99,21 +106,19 @@ def tile_attention_pb_kernel(tc, attn_out, hg_lin, x, Wg, bg, bhg, Wo, out):
         x_codes = [keep.tile([P, PASSES, N], U32, name="x_codes%d" % b, align_bytes=64) for b in range(B)]
         x_scales = [keep.tile([P, PASSES, N], U8, name="x_scales%d" % b, align_bytes=64) for b in range(B)]
 
-        def quantise_weight(raw, codes, scales, scalar_halves):
-            pieces = [(half, g) for half in range(2) for g in range(PASSES)]
+        def quantise_weight(raw, codes, scales):
+            pieces = [(half, g) for half in range(HALVES) for g in range(PASSES)]
             grouped = {}
             for i in range(len(pieces) + 1):
                 if i < len(pieces):
                     half, g = pieces[i]
                     grouped[i] = work.tile(
-                        [P, BANK * PACK], BF16, tag="w_grp", bufs=4, align_bytes=64, name="w_grp"
+                        [P, BANK * PACK], BF16, tag="w_grp", bufs=3, align_bytes=64, name="w_grp"
                     )
-                    dst = grouped[i][:].rearrange("p (c i t) -> p c t i", i=4, t=PACK)
-                    src = raw[:, g, :, half * BANK : (half + 1) * BANK].rearrange("p t (c i) -> p c t i", i=4)
-                    if half in scalar_halves:
-                        nc.scalar.copy(out=dst, in_=src)
-                    else:
-                        nc.vector.tensor_copy(out=dst, in_=src)
+                    nc.vector.tensor_copy(
+                        out=grouped[i][:].rearrange("p (c i t) -> p c t i", i=4, t=PACK),
+                        in_=raw[:, g, :, half * BANK : (half + 1) * BANK].rearrange("p t (c i) -> p c t i", i=4),
+                    )
                 if i > 0:
                     half, g = pieces[i - 1]
                     cols = slice(half * BANK, (half + 1) * BANK)
@@ -126,10 +131,10 @@ def tile_attention_pb_kernel(tc, attn_out, hg_lin, x, Wg, bg, bhg, Wo, out):
         def transpose_x(b):
             words = x_sb[b][:].bitcast(F32)
             for g in range(PASSES):
-                x_grp[(b, g)] = work.tile([P, N * PACK], BF16, tag="x_grp", align_bytes=64, name="x_grp")
+                x_grp[(b, g)] = work.tile([P, N * PACK], BF16, tag="x_grp", bufs=4, align_bytes=64, name="x_grp")
                 grouped_words = x_grp[(b, g)][:].bitcast(F32)
                 for jp in range(J // 2):
-                    xt = psum.tile([P, BANK], F32, tag="tr", bufs=3, name="xt")
+                    xt = psum.tile([P, BANK], F32, tag="tr", name="xt")
                     for u in range(2):
                         for jj in range(2):
                             first = (2 * jp + jj) * (DIM // 2) + g * (K_PASS // 2) + u * P
@@ -149,114 +154,123 @@ def tile_attention_pb_kernel(tc, attn_out, hg_lin, x, Wg, bg, bhg, Wo, out):
                     out=x_codes[b][:, g, :].bitcast(FP8X4), scales=x_scales[b][:, g, :], in_=x_grp[(b, g)][:]
                 )
 
-        o_sb = {}
-
-        def gate_heads(b):
-            for j in range(J):
-                o_sb[(b, j)] = work.tile([P, HD], F32, tag="o_sb", bufs=B * J, name="o_sb")
-                if b == 0:
-                    nc.vector.tensor_tensor(
-                        out=o_sb[(b, j)][:].rearrange("p (h d) -> p h d", h=H),
-                        in0=attn_sb[b][:, :, j, :],
-                        in1=head_gate[:, b * J + j, :].unsqueeze(2).to_broadcast([P, H, D]),
-                        op=ALU.mult,
-                    )
-                else:
-                    for h in range(H):
-                        nc.scalar.activation(
-                            out=o_sb[(b, j)][:, h * D : (h + 1) * D],
-                            in_=attn_sb[b][:, h, j, :],
-                            func=ACT.Copy,
-                            scale=head_gate[:, b * J + j, h : h + 1],
-                        )
-
         g_sb = {}
 
-        def feature_gate(b, g2):
-            g_sb[(b, g2)] = work.tile([P, PACK, N], F32, tag="g_sb", bufs=B * PASSES, name="g_sb")
-            for t in range(PACK):
-                m = g2 * PACK + t
-                rows = slice(m * P, (m + 1) * P)
-                z = psum.tile([P, N], F32, tag="z", bufs=3, name="z")
-                for g in range(PASSES):
-                    nc.tensor.matmul_mx(
-                        out=z[:],
-                        lhsT=wg_codes[:, g, rows].bitcast(FP8X4),
-                        lhsT_scale=wg_scales[:, g, rows],
-                        rhs=x_codes[b][:, g, :].bitcast(FP8X4),
-                        rhs_scale=x_scales[b][:, g, :],
-                        start=(g == 0),
-                        stop=(g == PASSES - 1),
+        def feature_gate(b):
+            for g2 in range(PASSES):
+                g_sb[(b, g2)] = work.tile([P, PACK, N], F32, tag="g_sb", bufs=B * PASSES, name="g_sb")
+                for t in range(PACK):
+                    m = g2 * PACK + t
+                    rows = slice(m * P, (m + 1) * P)
+                    z = psum.tile([P, N], F32, tag="mm", name="z")
+                    for g in range(PASSES):
+                        nc.tensor.matmul_mx(
+                            out=z[:],
+                            lhsT=wg_codes[:, g, rows].bitcast(FP8X4),
+                            lhsT_scale=wg_scales[:, g, rows],
+                            rhs=x_codes[b][:, g, :].bitcast(FP8X4),
+                            rhs_scale=x_scales[b][:, g, :],
+                            start=(g == 0),
+                            stop=(g == PASSES - 1),
+                        )
+                    nc.scalar.activation(
+                        out=g_sb[(b, g2)][:, t, :], in_=z[:], func=ACT.Sigmoid, bias=bg_col[:, m : m + 1]
                     )
-                nc.scalar.activation(
-                    out=g_sb[(b, g2)][:, t, :], in_=z[:], func=ACT.Sigmoid, bias=bg_col[:, m : m + 1]
+
+        o_sb = {}
+
+        def gate_heads(i):
+            b, j = divmod(i, J)
+            o_sb[i] = work.tile([P, HD], F32, tag="o_sb", bufs=GATE_AHEAD + 2, name="o_sb")
+            if i < VECTOR_GATED_TILES:
+                nc.vector.tensor_tensor(
+                    out=o_sb[i][:].rearrange("p (h d) -> p h d", h=H),
+                    in0=attn_sb[b][:, :, j, :],
+                    in1=head_gate[:, i, :].unsqueeze(2).to_broadcast([P, H, D]),
+                    op=ALU.mult,
+                )
+            else:
+                for h in range(H):
+                    nc.scalar.activation(
+                        out=o_sb[i][:, h * D : (h + 1) * D],
+                        in_=attn_sb[b][:, h, j, :],
+                        func=ACT.Copy,
+                        scale=head_gate[:, i, h : h + 1],
+                    )
+
+        o_t = {}
+
+        def transpose_o(i):
+            for g2 in range(PASSES):
+                o_t[(i, g2)] = psum.tile([P, BANK], F32, tag="tr", name="o_t")
+                for t in range(PACK):
+                    first = g2 * K_PASS + t * P
+                    nc.tensor.transpose(
+                        o_t[(i, g2)][:, t * P : (t + 1) * P], o_sb[i][:, first : first + P], ident_f32[:]
+                    )
+
+        y_grp = {}
+
+        def gate_features(i):
+            b, j = divmod(i, J)
+            y_grp[i] = work.tile([P, PASSES * P * PACK], BF16, tag="y_grp", bufs=3, align_bytes=64, name="y_grp")
+            for g2 in range(PASSES):
+                nc.vector.tensor_tensor(
+                    out=y_grp[i][:, g2 * P * PACK : (g2 + 1) * P * PACK].rearrange("p (c t) -> p c t", t=PACK),
+                    in0=o_t[(i, g2)][:].rearrange("p (t c) -> p c t", t=PACK),
+                    in1=g_sb[(b, g2)][:, :, j * P : (j + 1) * P].rearrange("p t c -> p c t"),
+                    op=ALU.mult,
                 )
 
         y_codes = {}
         y_scales = {}
 
-        def gated_value(b, jp):
-            grouped = work.tile([P, PASSES * PAIR * P * PACK], BF16, tag="y_grp", align_bytes=64)
-            for g2 in range(PASSES):
-                for jj in range(PAIR):
-                    j = PAIR * jp + jj
-                    ot = psum.tile([P, BANK], F32, tag="tr", bufs=3, name="ot")
-                    for t in range(PACK):
-                        first = g2 * K_PASS + t * P
-                        nc.tensor.transpose(
-                            ot[:, t * P : (t + 1) * P], o_sb[(b, j)][:, first : first + P], ident_f32[:]
-                        )
-                    piece = (g2 * PAIR + jj) * P * PACK
-                    nc.vector.tensor_tensor(
-                        out=grouped[:, piece : piece + P * PACK].rearrange("p (c t) -> p c t", t=PACK),
-                        in0=ot[:].rearrange("p (t c) -> p c t", t=PACK),
-                        in1=g_sb[(b, g2)][:, :, j * P : (j + 1) * P].rearrange("p t c -> p c t"),
-                        op=ALU.mult,
-                    )
-            y_codes[(b, jp)] = keep.tile([P, PASSES * PAIR * P], U32, name="y_codes%d%d" % (b, jp), align_bytes=64)
-            y_scales[(b, jp)] = keep.tile([P, PASSES * PAIR * P], U8, name="y_scales%d%d" % (b, jp), align_bytes=64)
-            nc.vector.quantize_mx(
-                out=y_codes[(b, jp)][:].bitcast(FP8X4), scales=y_scales[(b, jp)][:], in_=grouped[:]
-            )
+        def quantise_y(i):
+            y_codes[i] = work.tile([P, PASSES * P], U32, tag="y_codes", bufs=4, align_bytes=64, name="y_codes")
+            y_scales[i] = work.tile([P, PASSES * P], U8, tag="y_scales", bufs=4, align_bytes=64, name="y_scales")
+            nc.vector.quantize_mx(out=y_codes[i][:].bitcast(FP8X4), scales=y_scales[i][:], in_=y_grp[i][:])
 
-        def project(b, jp):
+        def project(i):
+            b, j = divmod(i, J)
             out_view = out[b].rearrange("(p j) c -> p j c", j=J)
-            for jj in range(PAIR):
-                for half in range(DIM // BANK):
-                    cols = slice(half * BANK, (half + 1) * BANK)
-                    acc = psum.tile([P, BANK], F32, tag="acc", name="acc")
-                    for g2 in range(PASSES):
-                        toks = slice((g2 * PAIR + jj) * P, (g2 * PAIR + jj + 1) * P)
-                        nc.tensor.matmul_mx(
-                            out=acc[:],
-                            lhsT=y_codes[(b, jp)][:, toks].bitcast(FP8X4),
-                            lhsT_scale=y_scales[(b, jp)][:, toks],
-                            rhs=wo_codes[:, g2, cols].bitcast(FP8X4),
-                            rhs_scale=wo_scales[:, g2, cols],
-                            start=(g2 == 0),
-                            stop=(g2 == PASSES - 1),
-                        )
-                    res = work.tile([P, BANK], F32, tag="res", bufs=6)
-                    nc.scalar.copy(out=res[:], in_=acc[:])
-                    nc.sync.dma_start(out=out_view[:, PAIR * jp + jj, cols], in_=res[:])
+            for half in range(HALVES):
+                cols = slice(half * BANK, (half + 1) * BANK)
+                acc = psum.tile([P, BANK], F32, tag="mm", name="acc")
+                for g2 in range(PASSES):
+                    toks = slice(g2 * P, (g2 + 1) * P)
+                    nc.tensor.matmul_mx(
+                        out=acc[:],
+                        lhsT=y_codes[i][:, toks].bitcast(FP8X4),
+                        lhsT_scale=y_scales[i][:, toks],
+                        rhs=wo_codes[:, g2, cols].bitcast(FP8X4),
+                        rhs_scale=wo_scales[:, g2, cols],
+                        start=(g2 == 0),
+                        stop=(g2 == PASSES - 1),
+                    )
+                res = work.tile([P, BANK], F32, tag="res", bufs=6)
+                nc.scalar.copy(out=res[:], in_=acc[:])
+                nc.sync.dma_start(out=out_view[:, j, cols], in_=res[:])
 
         transpose_x(0)
         quantise_x(0)
-        quantise_weight(wg_raw, wg_codes, wg_scales, (1,))
-        feature_gate(0, 0)
-        feature_gate(0, 1)
+        quantise_weight(wg_raw, wg_codes, wg_scales)
         transpose_x(1)
-        gate_heads(0)
         quantise_x(1)
-        gated_value(0, 0)
-        feature_gate(1, 0)
-        feature_gate(1, 1)
-        quantise_weight(wo_raw, wo_codes, wo_scales, ())
-        gate_heads(1)
-        gated_value(0, 1)
-        project(0, 0)
-        gated_value(1, 0)
-        project(0, 1)
-        gated_value(1, 1)
-        project(1, 0)
-        project(1, 1)
+        feature_gate(0)
+        feature_gate(1)
+        for i in range(GATE_AHEAD):
+            gate_heads(i)
+        quantise_weight(wo_raw, wo_codes, wo_scales)
+        for i in range(TRANSPOSE_AHEAD):
+            transpose_o(i)
+        for i in range(TILES + PROJECT_BEHIND):
+            if i + GATE_AHEAD < TILES:
+                gate_heads(i + GATE_AHEAD)
+            if i + TRANSPOSE_AHEAD < TILES:
+                transpose_o(i + TRANSPOSE_AHEAD)
+            if i < TILES:
+                gate_features(i)
+            if 0 <= i - QUANTISE_BEHIND < TILES:
+                quantise_y(i - QUANTISE_BEHIND)
+            if i >= PROJECT_BEHIND:
+                project(i - PROJECT_BEHIND)

@@ -27,6 +27,7 @@ HD = H * D
 PASSES = DIM // K_PASS
 BANK = 512
 HALVES = DIM // BANK
+BHG_PAD = 64
 
 GATE_AHEAD = 4
 TRANSPOSE_AHEAD = 2
@@ -47,14 +48,14 @@ def tile_attention_pb_kernel(tc, attn_out, hg_lin, x, Wg, bg, bhg, Wo, out):
         make_identity(nc, ident_f32[:])
         ident_bf16 = keep.tile([P, P], BF16, name="ident_bf16")
         make_identity(nc, ident_bf16[:])
+        ones = keep.tile([P, P], BF16, name="ones")
+        nc.vector.memset(ones[:], 1.0)
         bg_rows = keep.tile([P, P], BF16, name="bg_rows")
         nc.vector.memset(bg_rows[:], 0.0)
+        bhg_rows = keep.tile([P, BHG_PAD], BF16, name="bhg_rows")
+        nc.vector.memset(bhg_rows[:], 0.0)
 
         hg_sb = keep.tile([P, B, J * H], BF16, name="hg_sb")
-        nc.sync.dma_start(out=hg_sb[:], in_=hg_lin.rearrange("b (p j) h -> p b (j h)", j=J))
-        bhg_sb = keep.tile([P, H], BF16, name="bhg_sb")
-        nc.sync.dma_start(out=bhg_sb[:], in_=bhg.partition_broadcast(P))
-        nc.sync.dma_start(out=bg_rows[0 : HD // P, :], in_=bg.rearrange("(m p) -> m p", p=P))
 
         x_sb = [keep.tile([P, J * DIM], BF16, name="x_sb%d" % b) for b in range(B)]
         attn_sb = [keep.tile([P, H, J, D], BF16, name="attn_sb%d" % b) for b in range(B)]
@@ -74,6 +75,9 @@ def tile_attention_pb_kernel(tc, attn_out, hg_lin, x, Wg, bg, bhg, Wo, out):
         wo_view = Wo.rearrange("(g t p) c -> g p t c", g=PASSES, t=PACK)
 
         load_x(0)
+        nc.sync.dma_start(out=bg_rows[0 : HD // P, :], in_=bg.rearrange("(m p) -> m p", p=P))
+        nc.sync.dma_start(out=bhg_rows[0:1, 0:H], in_=bhg.rearrange("(o h) -> o h", o=1))
+        nc.sync.dma_start(out=hg_sb[:], in_=hg_lin.rearrange("b (p j) h -> p b (j h)", j=J))
         for g in range(PASSES):
             nc.sync.dma_start(
                 out=wg_raw[:, g].rearrange("q (u e) c -> q u (e c)", e=2), in_=wg_view[g]
@@ -84,20 +88,23 @@ def tile_attention_pb_kernel(tc, attn_out, hg_lin, x, Wg, bg, bhg, Wo, out):
             nc.sync.dma_start(out=wo_raw[:, g], in_=wo_view[g])
         load_attn(1)
 
-        hg_sum = keep.tile([P, TILES, H], F32, name="hg_sum")
-        nc.vector.tensor_tensor(
-            out=hg_sum[:],
-            in0=hg_sb[:].rearrange("p b (j h) -> p (b j) h", h=H),
-            in1=bhg_sb[:].unsqueeze(1).to_broadcast([P, TILES, H]),
-            op=ALU.add,
-        )
-        head_gate = keep.tile([P, TILES, H], F32, name="head_gate")
-        nc.scalar.activation(out=head_gate[:], in_=hg_sum[:], func=ACT.Sigmoid)
-
-        bg_t = psum.tile([P, P], BF16, tag="tr", name="bg_t")
-        nc.tensor.transpose(bg_t[:], bg_rows[:], ident_bf16[:])
         bg_col = keep.tile([P, HD // P], F32, name="bg_col")
-        nc.vector.tensor_copy(out=bg_col[:], in_=bg_t[:, 0 : HD // P])
+        head_gate = keep.tile([P, TILES, H], F32, name="head_gate")
+
+        def small_operands():
+            bg_t = psum.tile([P, P], BF16, tag="tr", name="bg_t")
+            nc.tensor.transpose(bg_t[:], bg_rows[:], ident_bf16[:])
+            nc.vector.tensor_copy(out=bg_col[:], in_=bg_t[:, 0 : HD // P])
+            bhg_all = psum.tile([P, BHG_PAD], F32, tag="tr", name="bhg_all")
+            nc.tensor.matmul(bhg_all[:], lhsT=ones[:], rhs=bhg_rows[:], start=True, stop=True)
+            hg_sum = keep.tile([P, TILES, H], F32, name="hg_sum")
+            nc.vector.tensor_tensor(
+                out=hg_sum[:],
+                in0=hg_sb[:].rearrange("p b (j h) -> p (b j) h", h=H),
+                in1=bhg_all[:, 0:H].unsqueeze(1).to_broadcast([P, TILES, H]),
+                op=ALU.add,
+            )
+            nc.scalar.activation(out=head_gate[:], in_=hg_sum[:], func=ACT.Sigmoid)
 
         wg_codes = keep.tile([P, PASSES, HD], U32, name="wg_codes", align_bytes=64)
         wg_scales = keep.tile([P, PASSES, HD], U8, name="wg_scales", align_bytes=64)
@@ -211,16 +218,16 @@ def tile_attention_pb_kernel(tc, attn_out, hg_lin, x, Wg, bg, bhg, Wo, out):
 
         y_grp = {}
 
-        def gate_features(i):
+        def gate_features(i, g2):
             b, j = divmod(i, J)
-            y_grp[i] = work.tile([P, PASSES * P * PACK], BF16, tag="y_grp", bufs=3, align_bytes=64, name="y_grp")
-            for g2 in range(PASSES):
-                nc.vector.tensor_tensor(
-                    out=y_grp[i][:, g2 * P * PACK : (g2 + 1) * P * PACK].rearrange("p (c t) -> p c t", t=PACK),
-                    in0=o_t[(i, g2)][:].rearrange("p (t c) -> p c t", t=PACK),
-                    in1=g_sb[(b, g2)][:, :, j * P : (j + 1) * P].rearrange("p t c -> p c t"),
-                    op=ALU.mult,
-                )
+            if g2 == 0:
+                y_grp[i] = work.tile([P, PASSES * P * PACK], BF16, tag="y_grp", bufs=3, align_bytes=64, name="y_grp")
+            nc.vector.tensor_tensor(
+                out=y_grp[i][:, g2 * P * PACK : (g2 + 1) * P * PACK].rearrange("p (c t) -> p c t", t=PACK),
+                in0=o_t[(i, g2)][:].rearrange("p (t c) -> p c t", t=PACK),
+                in1=g_sb[(b, g2)][:, :, j * P : (j + 1) * P].rearrange("p t c -> p c t"),
+                op=ALU.mult,
+            )
 
         y_codes = {}
         y_scales = {}
@@ -252,6 +259,7 @@ def tile_attention_pb_kernel(tc, attn_out, hg_lin, x, Wg, bg, bhg, Wo, out):
                 nc.sync.dma_start(out=out_view[:, j, cols], in_=res[:])
 
         transpose_x(0)
+        small_operands()
         quantise_x(0)
         quantise_weight(wg_raw, wg_codes, wg_scales)
         transpose_x(1)
@@ -269,8 +277,10 @@ def tile_attention_pb_kernel(tc, attn_out, hg_lin, x, Wg, bg, bhg, Wo, out):
             if i + TRANSPOSE_AHEAD < TILES:
                 transpose_o(i + TRANSPOSE_AHEAD)
             if i < TILES:
-                gate_features(i)
+                gate_features(i, 0)
             if 0 <= i - QUANTISE_BEHIND < TILES:
                 quantise_y(i - QUANTISE_BEHIND)
+            if i < TILES:
+                gate_features(i, 1)
             if i >= PROJECT_BEHIND:
                 project(i - PROJECT_BEHIND)

@@ -27,7 +27,6 @@ HD = H * D
 PASSES = DIM // K_PASS
 BANK = 512
 HALVES = DIM // BANK
-BHG_PAD = 64
 
 GATE_AHEAD = 4
 TRANSPOSE_AHEAD = 2
@@ -42,20 +41,19 @@ def tile_attention_pb_kernel(tc, attn_out, hg_lin, x, Wg, bg, bhg, Wo, out):
         keep = stack.enter_context(tc.tile_pool(name="keep", bufs=1))
         work = stack.enter_context(tc.tile_pool(name="work", bufs=2))
         psum = stack.enter_context(tc.psum_pool(name="psum", bufs=4))
-        stack.enter_context(tc.manual_schedule())
 
         ident_f32 = keep.tile([P, P], F32, name="ident_f32")
         make_identity(nc, ident_f32[:])
         ident_bf16 = keep.tile([P, P], BF16, name="ident_bf16")
         make_identity(nc, ident_bf16[:])
-        ones = keep.tile([P, P], BF16, name="ones")
-        nc.vector.memset(ones[:], 1.0)
         bg_rows = keep.tile([P, P], BF16, name="bg_rows")
         nc.vector.memset(bg_rows[:], 0.0)
-        bhg_rows = keep.tile([P, BHG_PAD], BF16, name="bhg_rows")
-        nc.vector.memset(bhg_rows[:], 0.0)
 
         hg_sb = keep.tile([P, B, J * H], BF16, name="hg_sb")
+        nc.sync.dma_start(out=hg_sb[:], in_=hg_lin.rearrange("b (p j) h -> p b (j h)", j=J))
+        bhg_sb = keep.tile([P, H], BF16, name="bhg_sb")
+        nc.sync.dma_start(out=bhg_sb[:], in_=bhg.partition_broadcast(P))
+        nc.sync.dma_start(out=bg_rows[0 : HD // P, :], in_=bg.rearrange("(m p) -> m p", p=P))
 
         x_sb = [keep.tile([P, J * DIM], BF16, name="x_sb%d" % b) for b in range(B)]
         attn_sb = [keep.tile([P, H, J, D], BF16, name="attn_sb%d" % b) for b in range(B)]
@@ -75,9 +73,6 @@ def tile_attention_pb_kernel(tc, attn_out, hg_lin, x, Wg, bg, bhg, Wo, out):
         wo_view = Wo.rearrange("(g t p) c -> g p t c", g=PASSES, t=PACK)
 
         load_x(0)
-        nc.sync.dma_start(out=bg_rows[0 : HD // P, :], in_=bg.rearrange("(m p) -> m p", p=P))
-        nc.sync.dma_start(out=bhg_rows[0:1, 0:H], in_=bhg.rearrange("(o h) -> o h", o=1))
-        nc.sync.dma_start(out=hg_sb[:], in_=hg_lin.rearrange("b (p j) h -> p b (j h)", j=J))
         for g in range(PASSES):
             nc.sync.dma_start(
                 out=wg_raw[:, g].rearrange("q (u e) c -> q u (e c)", e=2), in_=wg_view[g]
@@ -88,23 +83,20 @@ def tile_attention_pb_kernel(tc, attn_out, hg_lin, x, Wg, bg, bhg, Wo, out):
             nc.sync.dma_start(out=wo_raw[:, g], in_=wo_view[g])
         load_attn(1)
 
-        bg_col = keep.tile([P, HD // P], F32, name="bg_col")
+        hg_sum = keep.tile([P, TILES, H], F32, name="hg_sum")
+        nc.vector.tensor_tensor(
+            out=hg_sum[:],
+            in0=hg_sb[:].rearrange("p b (j h) -> p (b j) h", h=H),
+            in1=bhg_sb[:].unsqueeze(1).to_broadcast([P, TILES, H]),
+            op=ALU.add,
+        )
         head_gate = keep.tile([P, TILES, H], F32, name="head_gate")
+        nc.scalar.activation(out=head_gate[:], in_=hg_sum[:], func=ACT.Sigmoid)
 
-        def small_operands():
-            bg_t = psum.tile([P, P], BF16, tag="tr", name="bg_t")
-            nc.tensor.transpose(bg_t[:], bg_rows[:], ident_bf16[:])
-            nc.vector.tensor_copy(out=bg_col[:], in_=bg_t[:, 0 : HD // P])
-            bhg_all = psum.tile([P, BHG_PAD], F32, tag="tr", name="bhg_all")
-            nc.tensor.matmul(bhg_all[:], lhsT=ones[:], rhs=bhg_rows[:], start=True, stop=True)
-            hg_sum = keep.tile([P, TILES, H], F32, name="hg_sum")
-            nc.vector.tensor_tensor(
-                out=hg_sum[:],
-                in0=hg_sb[:].rearrange("p b (j h) -> p (b j) h", h=H),
-                in1=bhg_all[:, 0:H].unsqueeze(1).to_broadcast([P, TILES, H]),
-                op=ALU.add,
-            )
-            nc.scalar.activation(out=head_gate[:], in_=hg_sum[:], func=ACT.Sigmoid)
+        bg_t = psum.tile([P, P], BF16, tag="tr", name="bg_t")
+        nc.tensor.transpose(bg_t[:], bg_rows[:], ident_bf16[:])
+        bg_col = keep.tile([P, HD // P], F32, name="bg_col")
+        nc.vector.tensor_copy(out=bg_col[:], in_=bg_t[:, 0 : HD // P])
 
         wg_codes = keep.tile([P, PASSES, HD], U32, name="wg_codes", align_bytes=64)
         wg_scales = keep.tile([P, PASSES, HD], U8, name="wg_scales", align_bytes=64)
@@ -218,16 +210,16 @@ def tile_attention_pb_kernel(tc, attn_out, hg_lin, x, Wg, bg, bhg, Wo, out):
 
         y_grp = {}
 
-        def gate_features(i, g2):
+        def gate_features(i):
             b, j = divmod(i, J)
-            if g2 == 0:
-                y_grp[i] = work.tile([P, PASSES * P * PACK], BF16, tag="y_grp", bufs=3, align_bytes=64, name="y_grp")
-            nc.vector.tensor_tensor(
-                out=y_grp[i][:, g2 * P * PACK : (g2 + 1) * P * PACK].rearrange("p (c t) -> p c t", t=PACK),
-                in0=o_t[(i, g2)][:].rearrange("p (t c) -> p c t", t=PACK),
-                in1=g_sb[(b, g2)][:, :, j * P : (j + 1) * P].rearrange("p t c -> p c t"),
-                op=ALU.mult,
-            )
+            y_grp[i] = work.tile([P, PASSES * P * PACK], BF16, tag="y_grp", bufs=3, align_bytes=64, name="y_grp")
+            for g2 in range(PASSES):
+                nc.vector.tensor_tensor(
+                    out=y_grp[i][:, g2 * P * PACK : (g2 + 1) * P * PACK].rearrange("p (c t) -> p c t", t=PACK),
+                    in0=o_t[(i, g2)][:].rearrange("p (t c) -> p c t", t=PACK),
+                    in1=g_sb[(b, g2)][:, :, j * P : (j + 1) * P].rearrange("p t c -> p c t"),
+                    op=ALU.mult,
+                )
 
         y_codes = {}
         y_scales = {}
@@ -259,7 +251,6 @@ def tile_attention_pb_kernel(tc, attn_out, hg_lin, x, Wg, bg, bhg, Wo, out):
                 nc.sync.dma_start(out=out_view[:, j, cols], in_=res[:])
 
         transpose_x(0)
-        small_operands()
         quantise_x(0)
         quantise_weight(wg_raw, wg_codes, wg_scales)
         transpose_x(1)
@@ -277,10 +268,8 @@ def tile_attention_pb_kernel(tc, attn_out, hg_lin, x, Wg, bg, bhg, Wo, out):
             if i + TRANSPOSE_AHEAD < TILES:
                 transpose_o(i + TRANSPOSE_AHEAD)
             if i < TILES:
-                gate_features(i, 0)
+                gate_features(i)
             if 0 <= i - QUANTISE_BEHIND < TILES:
                 quantise_y(i - QUANTISE_BEHIND)
-            if i < TILES:
-                gate_features(i, 1)
             if i >= PROJECT_BEHIND:
                 project(i - PROJECT_BEHIND)

from contextlib import ExitStack

import concourse.mybir as mybir
from concourse.masks import make_identity

FLOPS = 2 * 2 * 1024 * 1024 * 1024

BF16 = mybir.dt.bfloat16
F32 = mybir.dt.float32
U32 = mybir.dt.uint32
U8 = mybir.dt.uint8
FP8X4 = mybir.dt.float8_e4m3fn_x4
ACT = mybir.ActivationFunctionType
ALU = mybir.AluOpType

P = 128
PACK = 4
K_PASS = P * PACK
B = 2
N = 512
J = N // P
TILES = B * J
DIM = 1024
H = 16
D = 64
HD = H * D
PASSES = DIM // K_PASS
BANK = 512
HALVES = DIM // BANK

GATE_AHEAD = 4
TRANSPOSE_AHEAD = 2
QUANTISE_BEHIND = 1
PROJECT_BEHIND = 2
VECTOR_GATED_TILES = 2


def tile_attention_pb_kernel(tc, attn_out, hg_lin, x, Wg, bg, bhg, Wo, out):
    nc = tc.nc
    with ExitStack() as stack:
        keep = stack.enter_context(tc.tile_pool(name="keep", bufs=1))
        work = stack.enter_context(tc.tile_pool(name="work", bufs=2))
        psum = stack.enter_context(tc.psum_pool(name="psum", bufs=4))

        ident_f32 = keep.tile([P, P], F32, name="ident_f32")
        make_identity(nc, ident_f32[:])
        ident_bf16 = keep.tile([P, P], BF16, name="ident_bf16")
        make_identity(nc, ident_bf16[:])
        bg_rows = keep.tile([P, P], BF16, name="bg_rows")
        nc.vector.memset(bg_rows[:], 0.0)

        hg_sb = keep.tile([P, B, J * H], BF16, name="hg_sb")
        nc.sync.dma_start(out=hg_sb[:], in_=hg_lin.rearrange("b (p j) h -> p b (j h)", j=J))
        bhg_sb = keep.tile([P, H], BF16, name="bhg_sb")
        nc.sync.dma_start(out=bhg_sb[:], in_=bhg.partition_broadcast(P))
        nc.sync.dma_start(out=bg_rows[0 : HD // P, :], in_=bg.rearrange("(m p) -> m p", p=P))

        x_sb = [keep.tile([P, J * DIM], BF16, name="x_sb%d" % b) for b in range(B)]
        attn_sb = [keep.tile([P, H, J, D], BF16, name="attn_sb%d" % b) for b in range(B)]
        wg_raw = keep.tile([P, PASSES, PACK, HD], BF16, name="wg_raw")
        wo_raw = keep.tile([P, PASSES, PACK, DIM], BF16, name="wo_raw")

        def load_x(b):
            nc.sync.dma_start(out=x_sb[b][:], in_=x[b].rearrange("(p j) k -> p (j k)", j=J))

        def load_attn(b):
            nc.sync.dma_start(
                out=attn_sb[b][:].rearrange("p h j d -> p h (j d)"),
                in_=attn_out[b].rearrange("h (p j) d -> p h (j d)", j=J),
            )

        wg_view = Wg.rearrange("(g u q e) c -> g q u (e c)", g=PASSES, u=2, e=2)
        wo_view = Wo.rearrange("(g t p) c -> g p t c", g=PASSES, t=PACK)

        load_x(0)
        for g in range(PASSES):
            nc.sync.dma_start(
                out=wg_raw[:, g].rearrange("q (u e) c -> q u (e c)", e=2), in_=wg_view[g]
            )
        load_x(1)
        load_attn(0)
        for g in range(PASSES):
            nc.sync.dma_start(out=wo_raw[:, g], in_=wo_view[g])
        load_attn(1)

        hg_sum = keep.tile([P, TILES, H], F32, name="hg_sum")
        nc.vector.tensor_tensor(
            out=hg_sum[:],
            in0=hg_sb[:].rearrange("p b (j h) -> p (b j) h", h=H),
            in1=bhg_sb[:].unsqueeze(1).to_broadcast([P, TILES, H]),
            op=ALU.add,
        )
        head_gate = keep.tile([P, TILES, H], F32, name="head_gate")
        nc.scalar.activation(out=head_gate[:], in_=hg_sum[:], func=ACT.Sigmoid)

        bg_t = psum.tile([P, P], BF16, tag="tr", name="bg_t")
        nc.tensor.transpose(bg_t[:], bg_rows[:], ident_bf16[:])
        bg_col = keep.tile([P, HD // P], F32, name="bg_col")
        nc.vector.tensor_copy(out=bg_col[:], in_=bg_t[:, 0 : HD // P])

        wg_codes = keep.tile([P, PASSES, HD], U32, name="wg_codes", align_bytes=64)
        wg_scales = keep.tile([P, PASSES, HD], U8, name="wg_scales", align_bytes=64)
        wo_codes = keep.tile([P, PASSES, DIM], U32, name="wo_codes", align_bytes=64)
        wo_scales = keep.tile([P, PASSES, DIM], U8, name="wo_scales", align_bytes=64)
        x_codes = [keep.tile([P, PASSES, N], U32, name="x_codes%d" % b, align_bytes=64) for b in range(B)]
        x_scales = [keep.tile([P, PASSES, N], U8, name="x_scales%d" % b, align_bytes=64) for b in range(B)]

        def quantise_weight(raw, codes, scales):
            pieces = [(half, g) for half in range(HALVES) for g in range(PASSES)]
            grouped = {}
            for i in range(len(pieces) + 1):
                if i < len(pieces):
                    half, g = pieces[i]
                    grouped[i] = work.tile(
                        [P, BANK * PACK], BF16, tag="w_grp", bufs=3, align_bytes=64, name="w_grp"
                    )
                    nc.vector.tensor_copy(
                        out=grouped[i][:].rearrange("p (c i t) -> p c t i", i=4, t=PACK),
                        in_=raw[:, g, :, half * BANK : (half + 1) * BANK].rearrange("p t (c i) -> p c t i", i=4),
                    )
                if i > 0:
                    half, g = pieces[i - 1]
                    cols = slice(half * BANK, (half + 1) * BANK)
                    nc.vector.quantize_mx(
                        out=codes[:, g, cols].bitcast(FP8X4), scales=scales[:, g, cols], in_=grouped[i - 1][:]
                    )

        x_grp = {}

        def transpose_x(b):
            words = x_sb[b][:].bitcast(F32)
            for g in range(PASSES):
                x_grp[(b, g)] = work.tile([P, N * PACK], BF16, tag="x_grp", bufs=4, align_bytes=64, name="x_grp")
                grouped_words = x_grp[(b, g)][:].bitcast(F32)
                for jp in range(J // 2):
                    xt = psum.tile([P, BANK], F32, tag="tr", name="xt")
                    for u in range(2):
                        for jj in range(2):
                            first = (2 * jp + jj) * (DIM // 2) + g * (K_PASS // 2) + u * P
                            nc.tensor.transpose(
                                xt[:, (2 * u + jj) * P : (2 * u + jj + 1) * P],
                                words[:, first : first + P],
                                ident_f32[:],
                            )
                    nc.scalar.copy(
                        out=grouped_words[:, jp * BANK : (jp + 1) * BANK].rearrange("q (c u) -> q c u", u=2),
                        in_=xt[:].rearrange("q (u c) -> q c u", u=2),
                    )

        def quantise_x(b):
            for g in range(PASSES):
                nc.vector.quantize_mx(
                    out=x_codes[b][:, g, :].bitcast(FP8X4), scales=x_scales[b][:, g, :], in_=x_grp[(b, g)][:]
                )

        g_sb = {}

        def feature_gate(b):
            for g2 in range(PASSES):
                g_sb[(b, g2)] = work.tile([P, PACK, N], F32, tag="g_sb", bufs=B * PASSES, name="g_sb")
                for t in range(PACK):
                    m = g2 * PACK + t
                    rows = slice(m * P, (m + 1) * P)
                    z = psum.tile([P, N], F32, tag="mm", name="z")
                    for g in range(PASSES):
                        nc.tensor.matmul_mx(
                            out=z[:],
                            lhsT=wg_codes[:, g, rows].bitcast(FP8X4),
                            lhsT_scale=wg_scales[:, g, rows],
                            rhs=x_codes[b][:, g, :].bitcast(FP8X4),
                            rhs_scale=x_scales[b][:, g, :],
                            start=(g == 0),
                            stop=(g == PASSES - 1),
                        )
                    nc.scalar.activation(
                        out=g_sb[(b, g2)][:, t, :], in_=z[:], func=ACT.Sigmoid, bias=bg_col[:, m : m + 1]
                    )

        o_sb = {}

        def gate_heads(i):
            b, j = divmod(i, J)
            o_sb[i] = work.tile([P, HD], F32, tag="o_sb", bufs=GATE_AHEAD + 2, name="o_sb")
            if i < VECTOR_GATED_TILES:
                nc.vector.tensor_tensor(
                    out=o_sb[i][:].rearrange("p (h d) -> p h d", h=H),
                    in0=attn_sb[b][:, :, j, :],
                    in1=head_gate[:, i, :].unsqueeze(2).to_broadcast([P, H, D]),
                    op=ALU.mult,
                )
            else:
                for h in range(H):
                    nc.scalar.activation(
                        out=o_sb[i][:, h * D : (h + 1) * D],
                        in_=attn_sb[b][:, h, j, :],
                        func=ACT.Copy,
                        scale=head_gate[:, i, h : h + 1],
                    )

        o_t = {}

        def transpose_o(i):
            for g2 in range(PASSES):
                o_t[(i, g2)] = psum.tile([P, BANK], F32, tag="tr", name="o_t")
                for t in range(PACK):
                    first = g2 * K_PASS + t * P
                    nc.tensor.transpose(
                        o_t[(i, g2)][:, t * P : (t + 1) * P], o_sb[i][:, first : first + P], ident_f32[:]
                    )

        y_grp = {}

        def gate_features(i):
            b, j = divmod(i, J)
            y_grp[i] = work.tile([P, PASSES * P * PACK], BF16, tag="y_grp", bufs=3, align_bytes=64, name="y_grp")
            for g2 in range(PASSES):
                nc.vector.tensor_tensor(
                    out=y_grp[i][:, g2 * P * PACK : (g2 + 1) * P * PACK].rearrange("p (c t) -> p c t", t=PACK),
                    in0=o_t[(i, g2)][:].rearrange("p (t c) -> p c t", t=PACK),
                    in1=g_sb[(b, g2)][:, :, j * P : (j + 1) * P].rearrange("p t c -> p c t"),
                    op=ALU.mult,
                )

        y_codes = {}
        y_scales = {}

        def quantise_y(i):
            y_codes[i] = work.tile([P, PASSES * P], U32, tag="y_codes", bufs=4, align_bytes=64, name="y_codes")
            y_scales[i] = work.tile([P, PASSES * P], U8, tag="y_scales", bufs=4, align_bytes=64, name="y_scales")
            nc.vector.quantize_mx(out=y_codes[i][:].bitcast(FP8X4), scales=y_scales[i][:], in_=y_grp[i][:])

        def project(i):
            b, j = divmod(i, J)
            out_view = out[b].rearrange("(p j) c -> p j c", j=J)
            for half in range(HALVES):
                cols = slice(half * BANK, (half + 1) * BANK)
                acc = psum.tile([P, BANK], F32, tag="mm", name="acc")
                for g2 in range(PASSES):
                    toks = slice(g2 * P, (g2 + 1) * P)
                    nc.tensor.matmul_mx(
                        out=acc[:],
                        lhsT=y_codes[i][:, toks].bitcast(FP8X4),
                        lhsT_scale=y_scales[i][:, toks],
                        rhs=wo_codes[:, g2, cols].bitcast(FP8X4),
                        rhs_scale=wo_scales[:, g2, cols],
                        start=(g2 == 0),
                        stop=(g2 == PASSES - 1),
                    )
                res = work.tile([P, BANK], F32, tag="res", bufs=6)
                nc.scalar.copy(out=res[:], in_=acc[:])
                nc.sync.dma_start(out=out_view[:, j, cols], in_=res[:])

        transpose_x(0)
        quantise_x(0)
        quantise_weight(wg_raw, wg_codes, wg_scales)
        transpose_x(1)
        quantise_x(1)
        feature_gate(0)
        feature_gate(1)
        for i in range(GATE_AHEAD):
            gate_heads(i)
        quantise_weight(wo_raw, wo_codes, wo_scales)
        for i in range(TRANSPOSE_AHEAD):
            transpose_o(i)
        for i in range(TILES + PROJECT_BEHIND):
            if i + GATE_AHEAD < TILES:
                gate_heads(i + GATE_AHEAD)
            if i + TRANSPOSE_AHEAD < TILES:
                transpose_o(i + TRANSPOSE_AHEAD)
            if i < TILES:
                gate_features(i)
            if 0 <= i - QUANTISE_BEHIND < TILES:
                quantise_y(i - QUANTISE_BEHIND)
            if i >= PROJECT_BEHIND:
                project(i - PROJECT_BEHIND)
